import numpy as np
import ml_dtypes

BF16 = ml_dtypes.bfloat16


def bf(x):
    return np.asarray(x, np.float32).astype(BF16)


def f32(x):
    return np.asarray(x, np.float32)


def f64(x):
    return np.asarray(x).astype(np.float64)


def striped(idx):
    return np.tile(idx.reshape(-1, 16).T, (8, 1))


C, HID, S, Q, DEG, N, RUN, K = 512, 256, 256, 256, 8, 2048, 128, 16
SLOPE = 0.1


def lrelu(v):
    return np.maximum(v, SLOPE * v)


def setup_inputs():
    idx = np.concatenate([np.random.permutation(S)[:RUN] for _ in range(K)])
    return {"x": f32(np.random.standard_normal((C, S))), "pe": f32(np.random.standard_normal((1, N))), "w1": bf(np.random.standard_normal((C, HID)) / np.sqrt(C)), "b1": f32(0.1 * np.random.standard_normal((HID, 1))), "w2": bf(np.random.standard_normal((HID, C)) / np.sqrt(HID)), "b2": f32(0.1 * np.random.standard_normal((C, 1))), "offs": striped(idx)}


def reference(x, pe, w1, b1, w2, b2, offs):
    idx = offs[:16].T.reshape(-1)
    p = np.exp(f64(pe)).reshape(Q, DEG)
    alpha = (p / p.sum(axis=1, keepdims=True)).reshape(1, N)
    neigh = (f64(x)[:, idx] * alpha).reshape(C, Q, DEG).sum(axis=2)
    hid = lrelu(f64(w1).T @ neigh + f64(b1))
    return np.maximum(f64(w2).T @ hid + f64(b2), 0.0)

@@ -1,0 +1,141 @@
+import concourse.masks as masks
+import concourse.mybir as mybir
+
+F32 = mybir.dt.float32
+BF16 = mybir.dt.bfloat16
+U16 = mybir.dt.uint16
+ALU = mybir.AluOpType
+ACT = mybir.ActivationFunctionType
+AX = mybir.AxisListType
+
+P = 128
+C, HID, S, Q, DEG = 512, 256, 256, 256, 8
+N = Q * DEG
+SLOPE = 0.1
+CB = C // P
+UB = HID // P
+PIECE = S
+PIECES = N // PIECE
+OFFS_COLS = PIECE // 16
+ROW = N // P
+CHUNK = 64
+CHUNKS = Q // CHUNK
+CHUNK_PIECES = CHUNK * DEG // PIECE
+
+FLOPS = 2 * C * N + 2 * Q * (C * HID + HID * C)
+
+
+def tile_timeconv_kernel(tc, x, pe, w1, b1, w2, b2, offs, out):
+    nc = tc.nc
+    with (
+        tc.tile_pool(name="held", bufs=1) as held,
+        tc.tile_pool(name="spread", bufs=2) as spread,
+        tc.tile_pool(name="products", bufs=3) as products,
+        tc.tile_pool(name="work", bufs=2) as work,
+        tc.psum_pool(name="alpha_psum", bufs=2) as alpha_psum,
+        tc.psum_pool(name="mlp_psum", bufs=2) as mlp_psum,
+    ):
+        offsets = held.tile([P, N // 16], U16, name="offsets")
+        nc.sync.dma_start(offsets[:], offs)
+        pe_rows = held.tile([P, ROW], F32, name="pe_rows")
+        nc.scalar.dma_start(pe_rows[:], pe.rearrange("o (p t) -> (o p) t", t=ROW))
+        x_blocks = []
+        for b in range(CB):
+            x_block = held.tile([P, S], F32, name=f"x_block{b}")
+            nc.sync.dma_start(x_block[:], x[b * P : (b + 1) * P, :])
+            x_blocks.append(x_block)
+        w1_sb = held.tile([P, CB, HID], BF16, name="w1_sb")
+        nc.scalar.dma_start(w1_sb[:], w1.rearrange("(b p) u -> p b u", p=P))
+        w2_sb = held.tile([P, UB, C], BF16, name="w2_sb")
+        nc.scalar.dma_start(w2_sb[:], w2.rearrange("(u p) c -> p u c", p=P))
+        b1_sb = held.tile([P, UB], F32, name="b1_sb")
+        b2_sb = held.tile([P, CB], F32, name="b2_sb")
+        with nc.allow_non_contiguous_dma(reason="one bias element for each partition"):
+            nc.sync.dma_start(b1_sb[:], b1.rearrange("(u p) o -> p (u o)", p=P))
+            nc.sync.dma_start(b2_sb[:], b2.rearrange("(b p) o -> p (b o)", p=P))
+
+        groups = ROW // DEG
+        ones = held.tile([P, P], F32, name="ones")
+        nc.vector.memset(ones[:], 1.0)
+        identity = held.tile([P, P], F32, name="identity")
+        masks.make_identity(nc, identity[:])
+        top = held.tile([P, groups], F32, name="top")
+        shifted = held.tile([P, groups, DEG], F32, name="shifted")
+        expd = held.tile([P, groups, DEG], F32, name="expd")
+        total = held.tile([P, groups], F32, name="total")
+        inverse = held.tile([P, groups], F32, name="inverse")
+        alpha_rows = held.tile([P, groups, DEG], F32, name="alpha_rows")
+        pe_groups = pe_rows[:].rearrange("p (g d) -> p g d", d=DEG)
+        nc.vector.reduce_max(top[:], pe_groups, axis=AX.X)
+        nc.vector.tensor_tensor(
+            shifted[:], pe_groups, top[:].unsqueeze(2).to_broadcast([P, groups, DEG]), ALU.subtract
+        )
+        nc.scalar.activation(expd[:], shifted[:], ACT.Exp)
+        nc.vector.reduce_sum(total[:], expd[:], axis=AX.X)
+        nc.vector.reciprocal(inverse[:], total[:])
+        nc.vector.tensor_tensor(
+            alpha_rows[:], expd[:], inverse[:].unsqueeze(2).to_broadcast([P, groups, DEG]), ALU.mult
+        )
+
+        rows_per_piece = PIECE // ROW
+        alpha_pieces = []
+        for r in range(PIECES):
+            diagonal = spread.tile([P, rows_per_piece, ROW], F32, name="diagonal")
+            nc.gpsimd.tensor_tensor(
+                diagonal[:],
+                identity[:, r * rows_per_piece : (r + 1) * rows_per_piece]
+                .unsqueeze(2)
+                .to_broadcast([P, rows_per_piece, ROW]),
+                alpha_rows[:].rearrange("p g d -> p (g d)").unsqueeze(1).to_broadcast([P, rows_per_piece, ROW]),
+                ALU.mult,
+            )
+            alpha_bank = alpha_psum.tile([P, PIECE], F32, name="alpha_bank")
+            nc.tensor.matmul(
+                alpha_bank[:], ones[:], diagonal[:].rearrange("p q t -> p (q t)"), start=True, stop=True
+            )
+            alpha_piece = held.tile([P, PIECE], F32, name=f"alpha_piece{r}")
+            nc.scalar.copy(alpha_piece[:], alpha_bank[:])
+            alpha_pieces.append(alpha_piece)
+
+        out_blocks = out.rearrange("(b p) m -> p b m", p=P)
+        for c in range(CHUNKS):
+            neigh = work.tile([P, CB, CHUNK], BF16, name="neigh")
+            for b in range(CB):
+                product = products.tile([P, CHUNK * DEG], F32, name="product")
+                for h in range(CHUNK_PIECES):
+                    r = c * CHUNK_PIECES + h
+                    nc.vector.tensor_tensor(
+                        product[:, h * PIECE : (h + 1) * PIECE],
+                        x_blocks[b][:].indirect(offsets[:, r * OFFS_COLS : (r + 1) * OFFS_COLS]),
+                        alpha_pieces[r][:],
+                        ALU.mult,
+                    )
+                with nc.allow_low_precision(reason="summed in float32, rounded once to bfloat16"):
+                    nc.vector.reduce_sum(
+                        neigh[:, b, :], product[:].rearrange("p (m d) -> p m d", d=DEG), axis=AX.X
+                    )
+
+            hid_bank = mlp_psum.tile([P, UB, CHUNK], F32, name="hid_bank")
+            for u in range(UB):
+                for b in range(CB):
+                    nc.tensor.matmul(
+                        hid_bank[:, u, :], w1_sb[:, b, u * P : (u + 1) * P], neigh[:, b, :],
+                        start=(b == 0), stop=(b == CB - 1),
+                    )
+            biased = work.tile([P, UB, CHUNK], F32, name="biased")
+            for u in range(UB):
+                nc.scalar.activation(biased[:, u, :], hid_bank[:, u, :], ACT.Identity, bias=b1_sb[:, u : u + 1])
+            hid = work.tile([P, UB, CHUNK], BF16, name="hid")
+            nc.vector.scalar_tensor_tensor(hid[:], biased[:], SLOPE, biased[:], op0=ALU.mult, op1=ALU.max)
+
+            out_bank = mlp_psum.tile([P, CB, CHUNK], F32, name="out_bank")
+            for b in range(CB):
+                for u in range(UB):
+                    nc.tensor.matmul(
+                        out_bank[:, b, :], w2_sb[:, u, b * P : (b + 1) * P], hid[:, u, :],
+                        start=(u == 0), stop=(u == UB - 1),
+                    )
+            result = work.tile([P, CB, CHUNK], F32, name="result")
+            for b in range(CB):
+                nc.scalar.activation(result[:, b, :], out_bank[:, b, :], ACT.Relu, bias=b2_sb[:, b : b + 1])
+            nc.sync.dma_start(out_blocks[:, :, c * CHUNK : (c + 1) * CHUNK], result[:])

@@ -30,9 +30,10 @@ def tile_timeconv_kernel(tc, x, pe, w1, b1, w2, b2, offs, out):
     with (
         tc.tile_pool(name="held", bufs=1) as held,
         tc.tile_pool(name="spread", bufs=2) as spread,
-        tc.tile_pool(name="products", bufs=3) as products,
+        tc.tile_pool(name="products", bufs=4) as products,
         tc.tile_pool(name="work", bufs=2) as work,
         tc.psum_pool(name="alpha_psum", bufs=2) as alpha_psum,
+        tc.psum_pool(name="sum_psum", bufs=2) as sum_psum,
         tc.psum_pool(name="mlp_psum", bufs=2) as mlp_psum,
     ):
         offsets = held.tile([P, N // 16], U16, name="offsets")
@@ -99,7 +100,7 @@ def tile_timeconv_kernel(tc, x, pe, w1, b1, w2, b2, offs, out):
 
         out_blocks = out.rearrange("(b p) m -> p b m", p=P)
         for c in range(CHUNKS):
-            neigh = work.tile([P, CB, CHUNK], BF16, name="neigh")
+            sum_bank = sum_psum.tile([P, CB, CHUNK], F32, name="sum_bank")
             for b in range(CB):
                 product = products.tile([P, CHUNK * DEG], F32, name="product")
                 for h in range(CHUNK_PIECES):
@@ -110,10 +111,13 @@ def tile_timeconv_kernel(tc, x, pe, w1, b1, w2, b2, offs, out):
                         alpha_pieces[r][:],
                         ALU.mult,
                     )
-                with nc.allow_low_precision(reason="summed in float32, rounded once to bfloat16"):
-                    nc.vector.reduce_sum(
-                        neigh[:, b, :], product[:].rearrange("p (m d) -> p m d", d=DEG), axis=AX.X
+                by_fan_in = product[:].rearrange("p (m d) -> p m d", d=DEG)
+                for d in range(DEG):
+                    nc.tensor.matmul(
+                        sum_bank[:, b, :], identity[:], by_fan_in[:, :, d], start=(d == 0), stop=(d == DEG - 1)
                     )
+            neigh = work.tile([P, CB, CHUNK], BF16, name="neigh")
+            nc.scalar.copy(neigh[:], sum_bank[:])
 
             hid_bank = mlp_psum.tile([P, UB, CHUNK], F32, name="hid_bank")
             for u in range(UB):

@@ -21,6 +21,7 @@ ROW = N // P
 CHUNK = 64
 CHUNKS = Q // CHUNK
 CHUNK_PIECES = CHUNK * DEG // PIECE
+POOL_BLOCKS = 3
 
 FLOPS = 2 * C * N + 2 * Q * (C * HID + HID * C)
 
@@ -30,10 +31,9 @@ def tile_timeconv_kernel(tc, x, pe, w1, b1, w2, b2, offs, out):
     with (
         tc.tile_pool(name="held", bufs=1) as held,
         tc.tile_pool(name="spread", bufs=2) as spread,
-        tc.tile_pool(name="products", bufs=4) as products,
+        tc.tile_pool(name="products", bufs=3) as products,
         tc.tile_pool(name="work", bufs=2) as work,
         tc.psum_pool(name="alpha_psum", bufs=2) as alpha_psum,
-        tc.psum_pool(name="sum_psum", bufs=2) as sum_psum,
         tc.psum_pool(name="mlp_psum", bufs=2) as mlp_psum,
     ):
         offsets = held.tile([P, N // 16], U16, name="offsets")
@@ -100,24 +100,27 @@ def tile_timeconv_kernel(tc, x, pe, w1, b1, w2, b2, offs, out):
 
         out_blocks = out.rearrange("(b p) m -> p b m", p=P)
         for c in range(CHUNKS):
-            sum_bank = sum_psum.tile([P, CB, CHUNK], F32, name="sum_bank")
+            product = products.tile([P, CB, CHUNK, DEG], F32, name="product")
+            neigh = work.tile([P, CB, CHUNK], BF16, name="neigh")
             for b in range(CB):
-                product = products.tile([P, CHUNK * DEG], F32, name="product")
+                entries = product[:, b, :, :].rearrange("p m d -> p (m d)")
                 for h in range(CHUNK_PIECES):
                     r = c * CHUNK_PIECES + h
                     nc.vector.tensor_tensor(
-                        product[:, h * PIECE : (h + 1) * PIECE],
+                        entries[:, h * PIECE : (h + 1) * PIECE],
                         x_blocks[b][:].indirect(offsets[:, r * OFFS_COLS : (r + 1) * OFFS_COLS]),
                         alpha_pieces[r][:],
                         ALU.mult,
                     )
-                by_fan_in = product[:].rearrange("p (m d) -> p m d", d=DEG)
-                for d in range(DEG):
-                    nc.tensor.matmul(
-                        sum_bank[:, b, :], identity[:], by_fan_in[:, :, d], start=(d == 0), stop=(d == DEG - 1)
-                    )
-            neigh = work.tile([P, CB, CHUNK], BF16, name="neigh")
-            nc.scalar.copy(neigh[:], sum_bank[:])
+            fours = work.tile([P, POOL_BLOCKS, CHUNK, 4], F32, name="fours")
+            twos = work.tile([P, POOL_BLOCKS, CHUNK, 2], F32, name="twos")
+            nc.gpsimd.tensor_tensor(
+                fours[:], product[:, :POOL_BLOCKS, :, 0:4], product[:, :POOL_BLOCKS, :, 4:8], ALU.add
+            )
+            nc.gpsimd.tensor_tensor(twos[:], fours[:, :, :, 0:2], fours[:, :, :, 2:4], ALU.add)
+            nc.gpsimd.tensor_tensor(neigh[:, :POOL_BLOCKS, :], twos[:, :, :, 0], twos[:, :, :, 1], ALU.add)
+            with nc.allow_low_precision(reason="summed in float32, rounded once to bfloat16"):
+                nc.vector.reduce_sum(neigh[:, POOL_BLOCKS:, :], product[:, POOL_BLOCKS:, :, :], axis=AX.X)
 
             hid_bank = mlp_psum.tile([P, UB, CHUNK], F32, name="hid_bank")
             for u in range(UB):

@@ -21,7 +21,8 @@ ROW = N // P
 CHUNK = 64
 CHUNKS = Q // CHUNK
 CHUNK_PIECES = CHUNK * DEG // PIECE
-POOL_BLOCKS = 3
+WARM_UP = 6
+PE_BLOCKS = 2
 
 FLOPS = 2 * C * N + 2 * Q * (C * HID + HID * C)
 
@@ -34,12 +35,13 @@ def tile_timeconv_kernel(tc, x, pe, w1, b1, w2, b2, offs, out):
         tc.tile_pool(name="products", bufs=3) as products,
         tc.tile_pool(name="work", bufs=2) as work,
         tc.psum_pool(name="alpha_psum", bufs=2) as alpha_psum,
+        tc.psum_pool(name="sum_psum", bufs=2) as sum_psum,
         tc.psum_pool(name="mlp_psum", bufs=2) as mlp_psum,
     ):
+        pe_rows = held.tile([P, ROW], F32, name="pe_rows")
+        nc.sync.dma_start(pe_rows[:], pe.rearrange("o (p t) -> (o p) t", t=ROW))
         offsets = held.tile([P, N // 16], U16, name="offsets")
         nc.sync.dma_start(offsets[:], offs)
-        pe_rows = held.tile([P, ROW], F32, name="pe_rows")
-        nc.scalar.dma_start(pe_rows[:], pe.rearrange("o (p t) -> (o p) t", t=ROW))
         x_blocks = []
         for b in range(CB):
             x_block = held.tile([P, S], F32, name=f"x_block{b}")
@@ -60,6 +62,9 @@ def tile_timeconv_kernel(tc, x, pe, w1, b1, w2, b2, offs, out):
         nc.vector.memset(ones[:], 1.0)
         identity = held.tile([P, P], F32, name="identity")
         masks.make_identity(nc, identity[:])
+        warm_bank = alpha_psum.tile([P, PIECE], F32, name="alpha_bank")
+        for w in range(WARM_UP):
+            nc.tensor.matmul(warm_bank[:, :P], ones[:], ones[:], start=True, stop=True)
         top = held.tile([P, groups], F32, name="top")
         shifted = held.tile([P, groups, DEG], F32, name="shifted")
         expd = held.tile([P, groups, DEG], F32, name="expd")
@@ -112,15 +117,14 @@ def tile_timeconv_kernel(tc, x, pe, w1, b1, w2, b2, offs, out):
                         alpha_pieces[r][:],
                         ALU.mult,
                     )
-            fours = work.tile([P, POOL_BLOCKS, CHUNK, 4], F32, name="fours")
-            twos = work.tile([P, POOL_BLOCKS, CHUNK, 2], F32, name="twos")
-            nc.gpsimd.tensor_tensor(
-                fours[:], product[:, :POOL_BLOCKS, :, 0:4], product[:, :POOL_BLOCKS, :, 4:8], ALU.add
-            )
-            nc.gpsimd.tensor_tensor(twos[:], fours[:, :, :, 0:2], fours[:, :, :, 2:4], ALU.add)
-            nc.gpsimd.tensor_tensor(neigh[:, :POOL_BLOCKS, :], twos[:, :, :, 0], twos[:, :, :, 1], ALU.add)
+            sum_bank = sum_psum.tile([P, PE_BLOCKS, CHUNK], F32, name="sum_bank")
+            for d in range(DEG):
+                nc.tensor.matmul(
+                    sum_bank[:], identity[:], product[:, :PE_BLOCKS, :, d], start=(d == 0), stop=(d == DEG - 1)
+                )
+            nc.scalar.copy(neigh[:, :PE_BLOCKS, :], sum_bank[:])
             with nc.allow_low_precision(reason="summed in float32, rounded once to bfloat16"):
-                nc.vector.reduce_sum(neigh[:, POOL_BLOCKS:, :], product[:, POOL_BLOCKS:, :, :], axis=AX.X)
+                nc.vector.reduce_sum(neigh[:, PE_BLOCKS:, :], product[:, PE_BLOCKS:, :, :], axis=AX.X)
 
             hid_bank = mlp_psum.tile([P, UB, CHUNK], F32, name="hid_bank")
             for u in range(UB):

@@ -21,8 +21,6 @@ ROW = N // P
 CHUNK = 64
 CHUNKS = Q // CHUNK
 CHUNK_PIECES = CHUNK * DEG // PIECE
-WARM_UP = 6
-PE_BLOCKS = 2
 
 FLOPS = 2 * C * N + 2 * Q * (C * HID + HID * C)
 
@@ -31,17 +29,16 @@ def tile_timeconv_kernel(tc, x, pe, w1, b1, w2, b2, offs, out):
     nc = tc.nc
     with (
         tc.tile_pool(name="held", bufs=1) as held,
-        tc.tile_pool(name="spread", bufs=2) as spread,
+        tc.tile_pool(name="spread", bufs=4) as spread,
         tc.tile_pool(name="products", bufs=3) as products,
         tc.tile_pool(name="work", bufs=2) as work,
         tc.psum_pool(name="alpha_psum", bufs=2) as alpha_psum,
-        tc.psum_pool(name="sum_psum", bufs=2) as sum_psum,
         tc.psum_pool(name="mlp_psum", bufs=2) as mlp_psum,
     ):
-        pe_rows = held.tile([P, ROW], F32, name="pe_rows")
-        nc.sync.dma_start(pe_rows[:], pe.rearrange("o (p t) -> (o p) t", t=ROW))
         offsets = held.tile([P, N // 16], U16, name="offsets")
         nc.sync.dma_start(offsets[:], offs)
+        pe_rows = held.tile([P, ROW], F32, name="pe_rows")
+        nc.scalar.dma_start(pe_rows[:], pe.rearrange("o (p t) -> (o p) t", t=ROW))
         x_blocks = []
         for b in range(CB):
             x_block = held.tile([P, S], F32, name=f"x_block{b}")
@@ -62,9 +59,6 @@ def tile_timeconv_kernel(tc, x, pe, w1, b1, w2, b2, offs, out):
         nc.vector.memset(ones[:], 1.0)
         identity = held.tile([P, P], F32, name="identity")
         masks.make_identity(nc, identity[:])
-        warm_bank = alpha_psum.tile([P, PIECE], F32, name="alpha_bank")
-        for w in range(WARM_UP):
-            nc.tensor.matmul(warm_bank[:, :P], ones[:], ones[:], start=True, stop=True)
         top = held.tile([P, groups], F32, name="top")
         shifted = held.tile([P, groups, DEG], F32, name="shifted")
         expd = held.tile([P, groups, DEG], F32, name="expd")
@@ -87,7 +81,7 @@ def tile_timeconv_kernel(tc, x, pe, w1, b1, w2, b2, offs, out):
         alpha_pieces = []
         for r in range(PIECES):
             diagonal = spread.tile([P, rows_per_piece, ROW], F32, name="diagonal")
-            nc.gpsimd.tensor_tensor(
+            nc.vector.tensor_tensor(
                 diagonal[:],
                 identity[:, r * rows_per_piece : (r + 1) * rows_per_piece]
                 .unsqueeze(2)
@@ -105,37 +99,32 @@ def tile_timeconv_kernel(tc, x, pe, w1, b1, w2, b2, offs, out):
 
         out_blocks = out.rearrange("(b p) m -> p b m", p=P)
         for c in range(CHUNKS):
-            product = products.tile([P, CB, CHUNK, DEG], F32, name="product")
+            product = products.tile([P, CB, CHUNK * DEG], F32, name="product")
             neigh = work.tile([P, CB, CHUNK], BF16, name="neigh")
-            for b in range(CB):
-                entries = product[:, b, :, :].rearrange("p m d -> p (m d)")
-                for h in range(CHUNK_PIECES):
-                    r = c * CHUNK_PIECES + h
+            hid_banks = [mlp_psum.tile([P, CHUNK], F32, name=f"hid_bank{u}") for u in range(UB)]
+            for h in range(CHUNK_PIECES):
+                r = c * CHUNK_PIECES + h
+                for b in range(CB):
                     nc.vector.tensor_tensor(
-                        entries[:, h * PIECE : (h + 1) * PIECE],
+                        product[:, b, h * PIECE : (h + 1) * PIECE],
                         x_blocks[b][:].indirect(offsets[:, r * OFFS_COLS : (r + 1) * OFFS_COLS]),
                         alpha_pieces[r][:],
                         ALU.mult,
                     )
-            sum_bank = sum_psum.tile([P, PE_BLOCKS, CHUNK], F32, name="sum_bank")
-            for d in range(DEG):
-                nc.tensor.matmul(
-                    sum_bank[:], identity[:], product[:, :PE_BLOCKS, :, d], start=(d == 0), stop=(d == DEG - 1)
-                )
-            nc.scalar.copy(neigh[:, :PE_BLOCKS, :], sum_bank[:])
-            with nc.allow_low_precision(reason="summed in float32, rounded once to bfloat16"):
-                nc.vector.reduce_sum(neigh[:, PE_BLOCKS:, :], product[:, PE_BLOCKS:, :, :], axis=AX.X)
-
-            hid_bank = mlp_psum.tile([P, UB, CHUNK], F32, name="hid_bank")
-            for u in range(UB):
-                for b in range(CB):
-                    nc.tensor.matmul(
-                        hid_bank[:, u, :], w1_sb[:, b, u * P : (u + 1) * P], neigh[:, b, :],
-                        start=(b == 0), stop=(b == CB - 1),
-                    )
+                    if h < CHUNK_PIECES - 1:
+                        continue
+                    with nc.allow_low_precision(reason="summed in float32, rounded once to bfloat16"):
+                        nc.vector.reduce_sum(
+                            neigh[:, b, :], product[:, b, :].rearrange("p (m d) -> p m d", d=DEG), axis=AX.X
+                        )
+                    for u in range(UB):
+                        nc.tensor.matmul(
+                            hid_banks[u][:], w1_sb[:, b, u * P : (u + 1) * P], neigh[:, b, :],
+                            start=(b == 0), stop=(b == CB - 1),
+                        )
             biased = work.tile([P, UB, CHUNK], F32, name="biased")
             for u in range(UB):
-                nc.scalar.activation(biased[:, u, :], hid_bank[:, u, :], ACT.Identity, bias=b1_sb[:, u : u + 1])
+                nc.scalar.activation(biased[:, u, :], hid_banks[u][:], ACT.Identity, bias=b1_sb[:, u : u + 1])
             hid = work.tile([P, UB, CHUNK], BF16, name="hid")
             nc.vector.scalar_tensor_tensor(hid[:], biased[:], SLOPE, biased[:], op0=ALU.mult, op1=ALU.max)
 

@@ -21,6 +21,7 @@ ROW = N // P
 CHUNK = 64
 CHUNKS = Q // CHUNK
 CHUNK_PIECES = CHUNK * DEG // PIECE
+VECTOR_BLOCKS = 3
 
 FLOPS = 2 * C * N + 2 * Q * (C * HID + HID * C)
 
@@ -111,17 +112,25 @@ def tile_timeconv_kernel(tc, x, pe, w1, b1, w2, b2, offs, out):
                         alpha_pieces[r][:],
                         ALU.mult,
                     )
-                    if h < CHUNK_PIECES - 1:
-                        continue
+            fours = work.tile([P, CHUNK * 4], F32, name="fours")
+            twos = work.tile([P, CHUNK * 2], F32, name="twos")
+            eights = product[:, VECTOR_BLOCKS, :].rearrange("p (i two) -> p i two", two=2)
+            nc.gpsimd.tensor_tensor(fours[:], eights[:, :, 0], eights[:, :, 1], ALU.add)
+            fours_pairs = fours[:].rearrange("p (i two) -> p i two", two=2)
+            nc.gpsimd.tensor_tensor(twos[:], fours_pairs[:, :, 0], fours_pairs[:, :, 1], ALU.add)
+            twos_pairs = twos[:].rearrange("p (i two) -> p i two", two=2)
+            nc.gpsimd.tensor_tensor(neigh[:, VECTOR_BLOCKS, :], twos_pairs[:, :, 0], twos_pairs[:, :, 1], ALU.add)
+            for b in range(CB):
+                if b < VECTOR_BLOCKS:
                     with nc.allow_low_precision(reason="summed in float32, rounded once to bfloat16"):
                         nc.vector.reduce_sum(
                             neigh[:, b, :], product[:, b, :].rearrange("p (m d) -> p m d", d=DEG), axis=AX.X
                         )
-                    for u in range(UB):
-                        nc.tensor.matmul(
-                            hid_banks[u][:], w1_sb[:, b, u * P : (u + 1) * P], neigh[:, b, :],
-                            start=(b == 0), stop=(b == CB - 1),
-                        )
+                for u in range(UB):
+                    nc.tensor.matmul(
+                        hid_banks[u][:], w1_sb[:, b, u * P : (u + 1) * P], neigh[:, b, :],
+                        start=(b == 0), stop=(b == CB - 1),
+                    )
             biased = work.tile([P, UB, CHUNK], F32, name="biased")
             for u in range(UB):
                 nc.scalar.activation(biased[:, u, :], hid_banks[u][:], ACT.Identity, bias=b1_sb[:, u : u + 1])

@@ -21,7 +21,6 @@ ROW = N // P
 CHUNK = 64
 CHUNKS = Q // CHUNK
 CHUNK_PIECES = CHUNK * DEG // PIECE
-VECTOR_BLOCKS = 3
 
 FLOPS = 2 * C * N + 2 * Q * (C * HID + HID * C)
 
@@ -30,7 +29,7 @@ def tile_timeconv_kernel(tc, x, pe, w1, b1, w2, b2, offs, out):
     nc = tc.nc
     with (
         tc.tile_pool(name="held", bufs=1) as held,
-        tc.tile_pool(name="spread", bufs=4) as spread,
+        tc.tile_pool(name="spread", bufs=8) as spread,
         tc.tile_pool(name="products", bufs=3) as products,
         tc.tile_pool(name="work", bufs=2) as work,
         tc.psum_pool(name="alpha_psum", bufs=2) as alpha_psum,
@@ -112,25 +111,17 @@ def tile_timeconv_kernel(tc, x, pe, w1, b1, w2, b2, offs, out):
                         alpha_pieces[r][:],
                         ALU.mult,
                     )
-            fours = work.tile([P, CHUNK * 4], F32, name="fours")
-            twos = work.tile([P, CHUNK * 2], F32, name="twos")
-            eights = product[:, VECTOR_BLOCKS, :].rearrange("p (i two) -> p i two", two=2)
-            nc.gpsimd.tensor_tensor(fours[:], eights[:, :, 0], eights[:, :, 1], ALU.add)
-            fours_pairs = fours[:].rearrange("p (i two) -> p i two", two=2)
-            nc.gpsimd.tensor_tensor(twos[:], fours_pairs[:, :, 0], fours_pairs[:, :, 1], ALU.add)
-            twos_pairs = twos[:].rearrange("p (i two) -> p i two", two=2)
-            nc.gpsimd.tensor_tensor(neigh[:, VECTOR_BLOCKS, :], twos_pairs[:, :, 0], twos_pairs[:, :, 1], ALU.add)
-            for b in range(CB):
-                if b < VECTOR_BLOCKS:
+                    if h < CHUNK_PIECES - 1:
+                        continue
                     with nc.allow_low_precision(reason="summed in float32, rounded once to bfloat16"):
                         nc.vector.reduce_sum(
                             neigh[:, b, :], product[:, b, :].rearrange("p (m d) -> p m d", d=DEG), axis=AX.X
                         )
-                for u in range(UB):
-                    nc.tensor.matmul(
-                        hid_banks[u][:], w1_sb[:, b, u * P : (u + 1) * P], neigh[:, b, :],
-                        start=(b == 0), stop=(b == CB - 1),
-                    )
+                    for u in range(UB):
+                        nc.tensor.matmul(
+                            hid_banks[u][:], w1_sb[:, b, u * P : (u + 1) * P], neigh[:, b, :],
+                            start=(b == 0), stop=(b == CB - 1),
+                        )
             biased = work.tile([P, UB, CHUNK], F32, name="biased")
             for u in range(UB):
                 nc.scalar.activation(biased[:, u, :], hid_banks[u][:], ACT.Identity, bias=b1_sb[:, u : u + 1])

@@ -21,6 +21,8 @@ ROW = N // P
 CHUNK = 64
 CHUNKS = Q // CHUNK
 CHUNK_PIECES = CHUNK * DEG // PIECE
+NODES = PIECE // DEG
+PE_BLOCKS = 3
 
 FLOPS = 2 * C * N + 2 * Q * (C * HID + HID * C)
 
@@ -30,9 +32,10 @@ def tile_timeconv_kernel(tc, x, pe, w1, b1, w2, b2, offs, out):
     with (
         tc.tile_pool(name="held", bufs=1) as held,
         tc.tile_pool(name="spread", bufs=8) as spread,
-        tc.tile_pool(name="products", bufs=3) as products,
+        tc.tile_pool(name="products", bufs=4) as products,
         tc.tile_pool(name="work", bufs=2) as work,
         tc.psum_pool(name="alpha_psum", bufs=2) as alpha_psum,
+        tc.psum_pool(name="sum_psum", bufs=2) as sum_psum,
         tc.psum_pool(name="mlp_psum", bufs=2) as mlp_psum,
     ):
         offsets = held.tile([P, N // 16], U16, name="offsets")
@@ -53,6 +56,11 @@ def tile_timeconv_kernel(tc, x, pe, w1, b1, w2, b2, offs, out):
         with nc.allow_non_contiguous_dma(reason="one bias element for each partition"):
             nc.sync.dma_start(b1_sb[:], b1.rearrange("(u p) o -> p (u o)", p=P))
             nc.sync.dma_start(b2_sb[:], b2.rearrange("(b p) o -> p (b o)", p=P))
+
+        minus_w2 = held.tile([P, UB, C], BF16, name="minus_w2")
+        nc.scalar.mul(minus_w2[:], w2_sb[:], -1.0)
+        minus_b1 = held.tile([P, UB], F32, name="minus_b1")
+        nc.scalar.mul(minus_b1[:], b1_sb[:], -SLOPE)
 
         groups = ROW // DEG
         ones = held.tile([P, P], F32, name="ones")
@@ -98,44 +106,64 @@ def tile_timeconv_kernel(tc, x, pe, w1, b1, w2, b2, offs, out):
             alpha_pieces.append(alpha_piece)
 
         out_blocks = out.rearrange("(b p) m -> p b m", p=P)
-        for c in range(CHUNKS):
-            product = products.tile([P, CB, CHUNK * DEG], F32, name="product")
-            neigh = work.tile([P, CB, CHUNK], BF16, name="neigh")
-            hid_banks = [mlp_psum.tile([P, CHUNK], F32, name=f"hid_bank{u}") for u in range(UB)]
-            for h in range(CHUNK_PIECES):
-                r = c * CHUNK_PIECES + h
+        neighs = []
+        hids = []
+        for r in range(PIECES + 2):
+            if r < PIECES:
+                c, h = divmod(r, CHUNK_PIECES)
+                if h == 0:
+                    neighs.append(work.tile([P, CB, CHUNK], BF16, name="neigh"))
+                neigh = neighs[c]
+                columns = slice(h * NODES, (h + 1) * NODES)
+                product = products.tile([P, CB, PIECE], F32, name="product")
                 for b in range(CB):
                     nc.vector.tensor_tensor(
-                        product[:, b, h * PIECE : (h + 1) * PIECE],
+                        product[:, b, :],
                         x_blocks[b][:].indirect(offsets[:, r * OFFS_COLS : (r + 1) * OFFS_COLS]),
                         alpha_pieces[r][:],
                         ALU.mult,
                     )
-                    if h < CHUNK_PIECES - 1:
-                        continue
-                    with nc.allow_low_precision(reason="summed in float32, rounded once to bfloat16"):
-                        nc.vector.reduce_sum(
-                            neigh[:, b, :], product[:, b, :].rearrange("p (m d) -> p m d", d=DEG), axis=AX.X
-                        )
-                    for u in range(UB):
+                terms = product[:].rearrange("p b (m d) -> p b m d", d=DEG)
+                sum_bank = sum_psum.tile([P, PE_BLOCKS, NODES], F32, name="sum_bank")
+                for d in range(DEG):
+                    nc.tensor.matmul(
+                        sum_bank[:], identity[:], terms[:, :PE_BLOCKS, :, d], start=(d == 0), stop=(d == DEG - 1)
+                    )
+                nc.scalar.copy(neigh[:, :PE_BLOCKS, columns], sum_bank[:])
+                with nc.allow_low_precision(reason="summed in float32, rounded once to bfloat16"):
+                    nc.vector.reduce_sum(neigh[:, PE_BLOCKS:, columns], terms[:, PE_BLOCKS:, :, :], axis=AX.X)
+
+            if r >= CHUNK_PIECES and r % CHUNK_PIECES == 0:
+                c = r // CHUNK_PIECES - 1
+                hid_bank = mlp_psum.tile([P, UB, CHUNK], F32, name="hid_bank")
+                for u in range(UB):
+                    for b in range(CB):
                         nc.tensor.matmul(
-                            hid_banks[u][:], w1_sb[:, b, u * P : (u + 1) * P], neigh[:, b, :],
+                            hid_bank[:, u, :], w1_sb[:, b, u * P : (u + 1) * P], neighs[c][:, b, :],
                             start=(b == 0), stop=(b == CB - 1),
                         )
-            biased = work.tile([P, UB, CHUNK], F32, name="biased")
-            for u in range(UB):
-                nc.scalar.activation(biased[:, u, :], hid_banks[u][:], ACT.Identity, bias=b1_sb[:, u : u + 1])
-            hid = work.tile([P, UB, CHUNK], BF16, name="hid")
-            nc.vector.scalar_tensor_tensor(hid[:], biased[:], SLOPE, biased[:], op0=ALU.mult, op1=ALU.max)
-
-            out_bank = mlp_psum.tile([P, CB, CHUNK], F32, name="out_bank")
-            for b in range(CB):
+                hid = work.tile([P, 2, UB, CHUNK], BF16, name="hid")
                 for u in range(UB):
-                    nc.tensor.matmul(
-                        out_bank[:, b, :], w2_sb[:, u, b * P : (b + 1) * P], hid[:, u, :],
-                        start=(u == 0), stop=(u == UB - 1),
+                    nc.scalar.activation(hid[:, 0, u, :], hid_bank[:, u, :], ACT.Relu, bias=b1_sb[:, u : u + 1])
+                    nc.scalar.activation(
+                        hid[:, 1, u, :], hid_bank[:, u, :], ACT.Relu, bias=minus_b1[:, u : u + 1], scale=-SLOPE
                     )
-            result = work.tile([P, CB, CHUNK], F32, name="result")
-            for b in range(CB):
-                nc.scalar.activation(result[:, b, :], out_bank[:, b, :], ACT.Relu, bias=b2_sb[:, b : b + 1])
-            nc.sync.dma_start(out_blocks[:, :, c * CHUNK : (c + 1) * CHUNK], result[:])
+                hids.append(hid)
+
+            if r >= CHUNK_PIECES + 1 and r % CHUNK_PIECES == 1:
+                c = r // CHUNK_PIECES - 1
+                out_bank = mlp_psum.tile([P, CB, CHUNK], F32, name="out_bank")
+                for b in range(CB):
+                    for u in range(UB):
+                        nc.tensor.matmul(
+                            out_bank[:, b, :], w2_sb[:, u, b * P : (b + 1) * P], hids[c][:, 0, u, :],
+                            start=(u == 0), stop=False,
+                        )
+                        nc.tensor.matmul(
+                            out_bank[:, b, :], minus_w2[:, u, b * P : (b + 1) * P], hids[c][:, 1, u, :],
+                            start=False, stop=(u == UB - 1),
+                        )
+                result = work.tile([P, CB, CHUNK], F32, name="result")
+                for b in range(CB):
+                    nc.scalar.activation(result[:, b, :], out_bank[:, b, :], ACT.Relu, bias=b2_sb[:, b : b + 1])
+                nc.sync.dma_start(out_blocks[:, :, c * CHUNK : (c + 1) * CHUNK], result[:])

@@ -21,8 +21,7 @@ ROW = N // P
 CHUNK = 64
 CHUNKS = Q // CHUNK
 CHUNK_PIECES = CHUNK * DEG // PIECE
-NODES = PIECE // DEG
-PE_BLOCKS = 3
+PE_CHUNKS = 2
 
 FLOPS = 2 * C * N + 2 * Q * (C * HID + HID * C)
 
@@ -32,11 +31,12 @@ def tile_timeconv_kernel(tc, x, pe, w1, b1, w2, b2, offs, out):
     with (
         tc.tile_pool(name="held", bufs=1) as held,
         tc.tile_pool(name="spread", bufs=8) as spread,
-        tc.tile_pool(name="products", bufs=4) as products,
-        tc.tile_pool(name="work", bufs=2) as work,
+        tc.tile_pool(name="products", bufs=CHUNKS) as products,
+        tc.tile_pool(name="work", bufs=3) as work,
         tc.psum_pool(name="alpha_psum", bufs=2) as alpha_psum,
-        tc.psum_pool(name="sum_psum", bufs=2) as sum_psum,
-        tc.psum_pool(name="mlp_psum", bufs=2) as mlp_psum,
+        tc.psum_pool(name="sum_psum", bufs=1) as sum_psum,
+        tc.psum_pool(name="hid_psum", bufs=1) as hid_psum,
+        tc.psum_pool(name="out_psum", bufs=2) as out_psum,
     ):
         offsets = held.tile([P, N // 16], U16, name="offsets")
         nc.sync.dma_start(offsets[:], offs)
@@ -108,59 +108,61 @@ def tile_timeconv_kernel(tc, x, pe, w1, b1, w2, b2, offs, out):
         out_blocks = out.rearrange("(b p) m -> p b m", p=P)
         neighs = []
         hids = []
-        for r in range(PIECES + 2):
-            if r < PIECES:
-                c, h = divmod(r, CHUNK_PIECES)
-                if h == 0:
-                    neighs.append(work.tile([P, CB, CHUNK], BF16, name="neigh"))
-                neigh = neighs[c]
-                columns = slice(h * NODES, (h + 1) * NODES)
-                product = products.tile([P, CB, PIECE], F32, name="product")
-                for b in range(CB):
-                    nc.vector.tensor_tensor(
-                        product[:, b, :],
-                        x_blocks[b][:].indirect(offsets[:, r * OFFS_COLS : (r + 1) * OFFS_COLS]),
-                        alpha_pieces[r][:],
-                        ALU.mult,
-                    )
+        for s in range(CHUNKS + 2):
+            if s < CHUNKS:
+                product = products.tile([P, CB, CHUNK * DEG], F32, name="product")
                 terms = product[:].rearrange("p b (m d) -> p b m d", d=DEG)
-                sum_bank = sum_psum.tile([P, PE_BLOCKS, NODES], F32, name="sum_bank")
-                for d in range(DEG):
-                    nc.tensor.matmul(
-                        sum_bank[:], identity[:], terms[:, :PE_BLOCKS, :, d], start=(d == 0), stop=(d == DEG - 1)
-                    )
-                nc.scalar.copy(neigh[:, :PE_BLOCKS, columns], sum_bank[:])
-                with nc.allow_low_precision(reason="summed in float32, rounded once to bfloat16"):
-                    nc.vector.reduce_sum(neigh[:, PE_BLOCKS:, columns], terms[:, PE_BLOCKS:, :, :], axis=AX.X)
-
-            if r >= CHUNK_PIECES and r % CHUNK_PIECES == 0:
-                c = r // CHUNK_PIECES - 1
-                hid_bank = mlp_psum.tile([P, UB, CHUNK], F32, name="hid_bank")
-                for u in range(UB):
+                neigh = work.tile([P, CB, CHUNK], BF16, name="neigh")
+                neighs.append(neigh)
+                for h in range(CHUNK_PIECES):
+                    r = s * CHUNK_PIECES + h
                     for b in range(CB):
-                        nc.tensor.matmul(
-                            hid_bank[:, u, :], w1_sb[:, b, u * P : (u + 1) * P], neighs[c][:, b, :],
-                            start=(b == 0), stop=(b == CB - 1),
+                        nc.vector.tensor_tensor(
+                            product[:, b, h * PIECE : (h + 1) * PIECE],
+                            x_blocks[b][:].indirect(offsets[:, r * OFFS_COLS : (r + 1) * OFFS_COLS]),
+                            alpha_pieces[r][:],
+                            ALU.mult,
                         )
-                hid = work.tile([P, 2, UB, CHUNK], BF16, name="hid")
-                for u in range(UB):
-                    nc.scalar.activation(hid[:, 0, u, :], hid_bank[:, u, :], ACT.Relu, bias=b1_sb[:, u : u + 1])
-                    nc.scalar.activation(
-                        hid[:, 1, u, :], hid_bank[:, u, :], ACT.Relu, bias=minus_b1[:, u : u + 1], scale=-SLOPE
-                    )
-                hids.append(hid)
+                        if s >= PE_CHUNKS and h == CHUNK_PIECES - 1:
+                            with nc.allow_low_precision(reason="summed in float32, rounded once to bfloat16"):
+                                nc.vector.reduce_sum(neigh[:, b, :], terms[:, b, :, :], axis=AX.X)
+                if s < PE_CHUNKS:
+                    sum_bank = sum_psum.tile([P, CB, CHUNK], F32, name="sum_bank")
+                    for d in range(DEG):
+                        nc.tensor.matmul(
+                            sum_bank[:], identity[:], terms[:, :, :, d], start=(d == 0), stop=(d == DEG - 1)
+                        )
+                    nc.scalar.copy(neigh[:], sum_bank[:])
 
-            if r >= CHUNK_PIECES + 1 and r % CHUNK_PIECES == 1:
-                c = r // CHUNK_PIECES - 1
-                out_bank = mlp_psum.tile([P, CB, CHUNK], F32, name="out_bank")
+            if 1 <= s <= CHUNKS:
+                neigh = neighs[s - 1]
+                hid_banks = [hid_psum.tile([P, CHUNK], F32, name=f"hid_bank{u}") for u in range(UB)]
                 for b in range(CB):
                     for u in range(UB):
                         nc.tensor.matmul(
-                            out_bank[:, b, :], w2_sb[:, u, b * P : (b + 1) * P], hids[c][:, 0, u, :],
+                            hid_banks[u][:], w1_sb[:, b, u * P : (u + 1) * P], neigh[:, b, :],
+                            start=(b == 0), stop=(b == CB - 1),
+                        )
+                hid = work.tile([P, 2, UB, CHUNK], BF16, name="hid")
+                hids.append(hid)
+                for u in range(UB):
+                    nc.scalar.activation(hid[:, 0, u, :], hid_banks[u][:], ACT.Relu, bias=b1_sb[:, u : u + 1])
+                    nc.scalar.activation(
+                        hid[:, 1, u, :], hid_banks[u][:], ACT.Relu, bias=minus_b1[:, u : u + 1], scale=-SLOPE
+                    )
+
+            if s >= 2:
+                c = s - 2
+                hid = hids[c]
+                out_bank = out_psum.tile([P, CB, CHUNK], F32, name="out_bank")
+                for b in range(CB):
+                    for u in range(UB):
+                        nc.tensor.matmul(
+                            out_bank[:, b, :], w2_sb[:, u, b * P : (b + 1) * P], hid[:, 0, u, :],
                             start=(u == 0), stop=False,
                         )
                         nc.tensor.matmul(
-                            out_bank[:, b, :], minus_w2[:, u, b * P : (b + 1) * P], hids[c][:, 1, u, :],
+                            out_bank[:, b, :], minus_w2[:, u, b * P : (b + 1) * P], hid[:, 1, u, :],
                             start=False, stop=(u == UB - 1),
                         )
                 result = work.tile([P, CB, CHUNK], F32, name="result")

@@ -21,7 +21,7 @@ ROW = N // P
 CHUNK = 64
 CHUNKS = Q // CHUNK
 CHUNK_PIECES = CHUNK * DEG // PIECE
-PE_CHUNKS = 2
+PE_CHUNKS = 1
 
 FLOPS = 2 * C * N + 2 * Q * (C * HID + HID * C)
 

@@ -21,7 +21,8 @@ ROW = N // P
 CHUNK = 64
 CHUNKS = Q // CHUNK
 CHUNK_PIECES = CHUNK * DEG // PIECE
-PE_CHUNKS = 1
+NODES = PIECE // DEG
+PE_PIECES = 3
 
 FLOPS = 2 * C * N + 2 * Q * (C * HID + HID * C)
 
@@ -31,7 +32,7 @@ def tile_timeconv_kernel(tc, x, pe, w1, b1, w2, b2, offs, out):
     with (
         tc.tile_pool(name="held", bufs=1) as held,
         tc.tile_pool(name="spread", bufs=8) as spread,
-        tc.tile_pool(name="products", bufs=CHUNKS) as products,
+        tc.tile_pool(name="products", bufs=PIECES) as products,
         tc.tile_pool(name="work", bufs=3) as work,
         tc.psum_pool(name="alpha_psum", bufs=2) as alpha_psum,
         tc.psum_pool(name="sum_psum", bufs=1) as sum_psum,
@@ -110,29 +111,32 @@ def tile_timeconv_kernel(tc, x, pe, w1, b1, w2, b2, offs, out):
         hids = []
         for s in range(CHUNKS + 2):
             if s < CHUNKS:
-                product = products.tile([P, CB, CHUNK * DEG], F32, name="product")
-                terms = product[:].rearrange("p b (m d) -> p b m d", d=DEG)
                 neigh = work.tile([P, CB, CHUNK], BF16, name="neigh")
                 neighs.append(neigh)
                 for h in range(CHUNK_PIECES):
                     r = s * CHUNK_PIECES + h
+                    columns = slice(h * NODES, (h + 1) * NODES)
+                    product = products.tile([P, CB, PIECE], F32, name="product")
+                    terms = product[:].rearrange("p b (m d) -> p b m d", d=DEG)
                     for b in range(CB):
                         nc.vector.tensor_tensor(
-                            product[:, b, h * PIECE : (h + 1) * PIECE],
+                            product[:, b, :],
                             x_blocks[b][:].indirect(offsets[:, r * OFFS_COLS : (r + 1) * OFFS_COLS]),
                             alpha_pieces[r][:],
                             ALU.mult,
                         )
-                        if s >= PE_CHUNKS and h == CHUNK_PIECES - 1:
+                        if r >= PE_PIECES and b % 2 == 1:
                             with nc.allow_low_precision(reason="summed in float32, rounded once to bfloat16"):
-                                nc.vector.reduce_sum(neigh[:, b, :], terms[:, b, :, :], axis=AX.X)
-                if s < PE_CHUNKS:
-                    sum_bank = sum_psum.tile([P, CB, CHUNK], F32, name="sum_bank")
-                    for d in range(DEG):
-                        nc.tensor.matmul(
-                            sum_bank[:], identity[:], terms[:, :, :, d], start=(d == 0), stop=(d == DEG - 1)
-                        )
-                    nc.scalar.copy(neigh[:], sum_bank[:])
+                                nc.vector.reduce_sum(
+                                    neigh[:, b - 1 : b + 1, columns], terms[:, b - 1 : b + 1, :, :], axis=AX.X
+                                )
+                    if r < PE_PIECES:
+                        sum_bank = sum_psum.tile([P, CB, NODES], F32, name="sum_bank")
+                        for d in range(DEG):
+                            nc.tensor.matmul(
+                                sum_bank[:], identity[:], terms[:, :, :, d], start=(d == 0), stop=(d == DEG - 1)
+                            )
+                        nc.scalar.copy(neigh[:, :, columns], sum_bank[:])
 
             if 1 <= s <= CHUNKS:
                 neigh = neighs[s - 1]

@@ -22,7 +22,7 @@ CHUNK = 64
 CHUNKS = Q // CHUNK
 CHUNK_PIECES = CHUNK * DEG // PIECE
 NODES = PIECE // DEG
-PE_PIECES = 3
+PE_PIECES = 5
 
 FLOPS = 2 * C * N + 2 * Q * (C * HID + HID * C)
 
@@ -33,6 +33,7 @@ def tile_timeconv_kernel(tc, x, pe, w1, b1, w2, b2, offs, out):
         tc.tile_pool(name="held", bufs=1) as held,
         tc.tile_pool(name="spread", bufs=8) as spread,
         tc.tile_pool(name="products", bufs=PIECES) as products,
+        tc.tile_pool(name="pairs", bufs=2) as pairs,
         tc.tile_pool(name="work", bufs=3) as work,
         tc.psum_pool(name="alpha_psum", bufs=2) as alpha_psum,
         tc.psum_pool(name="sum_psum", bufs=1) as sum_psum,
@@ -109,6 +110,7 @@ def tile_timeconv_kernel(tc, x, pe, w1, b1, w2, b2, offs, out):
         out_blocks = out.rearrange("(b p) m -> p b m", p=P)
         neighs = []
         hids = []
+        first_levels = []
         for s in range(CHUNKS + 2):
             if s < CHUNKS:
                 neigh = work.tile([P, CB, CHUNK], BF16, name="neigh")
@@ -131,12 +133,21 @@ def tile_timeconv_kernel(tc, x, pe, w1, b1, w2, b2, offs, out):
                                     neigh[:, b - 1 : b + 1, columns], terms[:, b - 1 : b + 1, :, :], axis=AX.X
                                 )
                     if r < PE_PIECES:
-                        sum_bank = sum_psum.tile([P, CB, NODES], F32, name="sum_bank")
-                        for d in range(DEG):
+                        pair_bank = sum_psum.tile([P, CB, NODES, 2], F32, name="pair_bank")
+                        for i in range(DEG // 2):
                             nc.tensor.matmul(
-                                sum_bank[:], identity[:], terms[:, :, :, d], start=(d == 0), stop=(d == DEG - 1)
+                                pair_bank[:], identity[:], terms[:, :, :, 2 * i : 2 * i + 2],
+                                start=(i == 0), stop=(i == DEG // 2 - 1),
                             )
-                        nc.scalar.copy(neigh[:, :, columns], sum_bank[:])
+                        pair = pairs.tile([P, CB, NODES, 2], F32, name="pair")
+                        nc.scalar.copy(pair[:], pair_bank[:])
+                        first_levels.append((pair, neigh, columns))
+                    if 1 <= r <= PE_PIECES:
+                        pair, pair_neigh, pair_columns = first_levels[r - 1]
+                        sum_bank = sum_psum.tile([P, CB, NODES], F32, name="sum_bank")
+                        for e in range(2):
+                            nc.tensor.matmul(sum_bank[:], identity[:], pair[:, :, :, e], start=(e == 0), stop=(e == 1))
+                        nc.scalar.copy(pair_neigh[:, :, pair_columns], sum_bank[:])
 
             if 1 <= s <= CHUNKS:
                 neigh = neighs[s - 1]

@@ -40,19 +40,24 @@ def tile_timeconv_kernel(tc, x, pe, w1, b1, w2, b2, offs, out):
         tc.psum_pool(name="hid_psum", bufs=1) as hid_psum,
         tc.psum_pool(name="out_psum", bufs=2) as out_psum,
     ):
+        warm = held.tile([P, 1], F32, name="warm")
+        nc.vector.memset(warm[:], 0.0)
+        warmed = held.tile([P, 1], F32, name="warmed")
+        nc.scalar.activation(warmed[:], warm[:], ACT.Exp)
+
+        pe_rows = held.tile([P, ROW], F32, name="pe_rows")
+        nc.sync.dma_start(pe_rows[:], pe.rearrange("o (p t) -> (o p) t", t=ROW))
         offsets = held.tile([P, N // 16], U16, name="offsets")
         nc.sync.dma_start(offsets[:], offs)
-        pe_rows = held.tile([P, ROW], F32, name="pe_rows")
-        nc.scalar.dma_start(pe_rows[:], pe.rearrange("o (p t) -> (o p) t", t=ROW))
         x_blocks = []
         for b in range(CB):
             x_block = held.tile([P, S], F32, name=f"x_block{b}")
             nc.sync.dma_start(x_block[:], x[b * P : (b + 1) * P, :])
             x_blocks.append(x_block)
         w1_sb = held.tile([P, CB, HID], BF16, name="w1_sb")
-        nc.scalar.dma_start(w1_sb[:], w1.rearrange("(b p) u -> p b u", p=P))
+        nc.sync.dma_start(w1_sb[:], w1.rearrange("(b p) u -> p b u", p=P))
         w2_sb = held.tile([P, UB, C], BF16, name="w2_sb")
-        nc.scalar.dma_start(w2_sb[:], w2.rearrange("(u p) c -> p u c", p=P))
+        nc.sync.dma_start(w2_sb[:], w2.rearrange("(u p) c -> p u c", p=P))
         b1_sb = held.tile([P, UB], F32, name="b1_sb")
         b2_sb = held.tile([P, CB], F32, name="b2_sb")
         with nc.allow_non_contiguous_dma(reason="one bias element for each partition"):
@@ -69,19 +74,18 @@ def tile_timeconv_kernel(tc, x, pe, w1, b1, w2, b2, offs, out):
         nc.vector.memset(ones[:], 1.0)
         identity = held.tile([P, P], F32, name="identity")
         masks.make_identity(nc, identity[:])
-        top = held.tile([P, groups], F32, name="top")
-        shifted = held.tile([P, groups, DEG], F32, name="shifted")
+        minus_top = held.tile([P, groups], F32, name="minus_top")
         expd = held.tile([P, groups, DEG], F32, name="expd")
         total = held.tile([P, groups], F32, name="total")
         inverse = held.tile([P, groups], F32, name="inverse")
         alpha_rows = held.tile([P, groups, DEG], F32, name="alpha_rows")
         pe_groups = pe_rows[:].rearrange("p (g d) -> p g d", d=DEG)
-        nc.vector.reduce_max(top[:], pe_groups, axis=AX.X)
-        nc.vector.tensor_tensor(
-            shifted[:], pe_groups, top[:].unsqueeze(2).to_broadcast([P, groups, DEG]), ALU.subtract
-        )
-        nc.scalar.activation(expd[:], shifted[:], ACT.Exp)
-        nc.vector.reduce_sum(total[:], expd[:], axis=AX.X)
+        nc.vector.reduce_max(minus_top[:], pe_groups, axis=AX.X, negate=True)
+        for g in range(groups):
+            nc.scalar.activation(
+                expd[:, g, :], pe_groups[:, g, :], ACT.Exp,
+                bias=minus_top[:, g : g + 1], accum_out=total[:, g : g + 1],
+            )
         nc.vector.reciprocal(inverse[:], total[:])
         nc.vector.tensor_tensor(
             alpha_rows[:], expd[:], inverse[:].unsqueeze(2).to_broadcast([P, groups, DEG]), ALU.mult

@@ -49,6 +49,8 @@ def tile_timeconv_kernel(tc, x, pe, w1, b1, w2, b2, offs, out):
         nc.sync.dma_start(pe_rows[:], pe.rearrange("o (p t) -> (o p) t", t=ROW))
         offsets = held.tile([P, N // 16], U16, name="offsets")
         nc.sync.dma_start(offsets[:], offs)
+        w2_sb = held.tile([P, UB, C], BF16, name="w2_sb")
+        nc.sync.dma_start(w2_sb[:], w2.rearrange("(u p) c -> p u c", p=P))
         x_blocks = []
         for b in range(CB):
             x_block = held.tile([P, S], F32, name=f"x_block{b}")
@@ -56,8 +58,6 @@ def tile_timeconv_kernel(tc, x, pe, w1, b1, w2, b2, offs, out):
             x_blocks.append(x_block)
         w1_sb = held.tile([P, CB, HID], BF16, name="w1_sb")
         nc.sync.dma_start(w1_sb[:], w1.rearrange("(b p) u -> p b u", p=P))
-        w2_sb = held.tile([P, UB, C], BF16, name="w2_sb")
-        nc.sync.dma_start(w2_sb[:], w2.rearrange("(u p) c -> p u c", p=P))
         b1_sb = held.tile([P, UB], F32, name="b1_sb")
         b2_sb = held.tile([P, CB], F32, name="b2_sb")
         with nc.allow_non_contiguous_dma(reason="one bias element for each partition"):
@@ -67,7 +67,7 @@ def tile_timeconv_kernel(tc, x, pe, w1, b1, w2, b2, offs, out):
         minus_w2 = held.tile([P, UB, C], BF16, name="minus_w2")
         nc.scalar.mul(minus_w2[:], w2_sb[:], -1.0)
         minus_b1 = held.tile([P, UB], F32, name="minus_b1")
-        nc.scalar.mul(minus_b1[:], b1_sb[:], -SLOPE)
+        nc.gpsimd.tensor_scalar_mul(minus_b1[:], b1_sb[:], -SLOPE)
 
         groups = ROW // DEG
         ones = held.tile([P, P], F32, name="ones")
@@ -143,14 +143,14 @@ def tile_timeconv_kernel(tc, x, pe, w1, b1, w2, b2, offs, out):
                                 pair_bank[:], identity[:], terms[:, :, :, 2 * i : 2 * i + 2],
                                 start=(i == 0), stop=(i == DEG // 2 - 1),
                             )
-                        pair = pairs.tile([P, CB, NODES, 2], F32, name="pair")
-                        nc.scalar.copy(pair[:], pair_bank[:])
+                        pair = pairs.tile([P, 2, CB, NODES], F32, name="pair")
+                        nc.scalar.copy(pair[:], pair_bank[:].rearrange("p b m e -> p e b m"))
                         first_levels.append((pair, neigh, columns))
                     if 1 <= r <= PE_PIECES:
                         pair, pair_neigh, pair_columns = first_levels[r - 1]
                         sum_bank = sum_psum.tile([P, CB, NODES], F32, name="sum_bank")
                         for e in range(2):
-                            nc.tensor.matmul(sum_bank[:], identity[:], pair[:, :, :, e], start=(e == 0), stop=(e == 1))
+                            nc.tensor.matmul(sum_bank[:], identity[:], pair[:, e, :, :], start=(e == 0), stop=(e == 1))
                         nc.scalar.copy(pair_neigh[:, :, pair_columns], sum_bank[:])
 
             if 1 <= s <= CHUNKS:

import concourse.masks as masks
import concourse.mybir as mybir

F32 = mybir.dt.float32
BF16 = mybir.dt.bfloat16
U16 = mybir.dt.uint16
ALU = mybir.AluOpType
ACT = mybir.ActivationFunctionType
AX = mybir.AxisListType

P = 128
C, HID, S, Q, DEG = 512, 256, 256, 256, 8
N = Q * DEG
SLOPE = 0.1
CB = C // P
UB = HID // P
PIECE = S
PIECES = N // PIECE
OFFS_COLS = PIECE // 16
ROW = N // P
CHUNK = 64
CHUNKS = Q // CHUNK
CHUNK_PIECES = CHUNK * DEG // PIECE
NODES = PIECE // DEG
PE_PIECES = 5

FLOPS = 2 * C * N + 2 * Q * (C * HID + HID * C)


def tile_timeconv_kernel(tc, x, pe, w1, b1, w2, b2, offs, out):
    nc = tc.nc
    with (
        tc.tile_pool(name="held", bufs=1) as held,
        tc.tile_pool(name="spread", bufs=8) as spread,
        tc.tile_pool(name="products", bufs=PIECES) as products,
        tc.tile_pool(name="pairs", bufs=2) as pairs,
        tc.tile_pool(name="work", bufs=3) as work,
        tc.psum_pool(name="alpha_psum", bufs=2) as alpha_psum,
        tc.psum_pool(name="sum_psum", bufs=1) as sum_psum,
        tc.psum_pool(name="hid_psum", bufs=1) as hid_psum,
        tc.psum_pool(name="out_psum", bufs=2) as out_psum,
    ):
        warm = held.tile([P, 1], F32, name="warm")
        nc.vector.memset(warm[:], 0.0)
        warmed = held.tile([P, 1], F32, name="warmed")
        nc.scalar.activation(warmed[:], warm[:], ACT.Exp)

        pe_rows = held.tile([P, ROW], F32, name="pe_rows")
        nc.sync.dma_start(pe_rows[:], pe.rearrange("o (p t) -> (o p) t", t=ROW))
        offsets = held.tile([P, N // 16], U16, name="offsets")
        nc.sync.dma_start(offsets[:], offs)
        w2_sb = held.tile([P, UB, C], BF16, name="w2_sb")
        nc.sync.dma_start(w2_sb[:], w2.rearrange("(u p) c -> p u c", p=P))
        x_blocks = []
        for b in range(CB):
            x_block = held.tile([P, S], F32, name=f"x_block{b}")
            nc.sync.dma_start(x_block[:], x[b * P : (b + 1) * P, :])
            x_blocks.append(x_block)
        w1_sb = held.tile([P, CB, HID], BF16, name="w1_sb")
        nc.sync.dma_start(w1_sb[:], w1.rearrange("(b p) u -> p b u", p=P))
        b1_sb = held.tile([P, UB], F32, name="b1_sb")
        b2_sb = held.tile([P, CB], F32, name="b2_sb")
        with nc.allow_non_contiguous_dma(reason="one bias element for each partition"):
            nc.sync.dma_start(b1_sb[:], b1.rearrange("(u p) o -> p (u o)", p=P))
            nc.sync.dma_start(b2_sb[:], b2.rearrange("(b p) o -> p (b o)", p=P))

        minus_w2 = held.tile([P, UB, C], BF16, name="minus_w2")
        nc.scalar.mul(minus_w2[:], w2_sb[:], -1.0)
        minus_b1 = held.tile([P, UB], F32, name="minus_b1")
        nc.gpsimd.tensor_scalar_mul(minus_b1[:], b1_sb[:], -SLOPE)

        groups = ROW // DEG
        ones = held.tile([P, P], F32, name="ones")
        nc.vector.memset(ones[:], 1.0)
        identity = held.tile([P, P], F32, name="identity")
        masks.make_identity(nc, identity[:])
        minus_top = held.tile([P, groups], F32, name="minus_top")
        expd = held.tile([P, groups, DEG], F32, name="expd")
        total = held.tile([P, groups], F32, name="total")
        inverse = held.tile([P, groups], F32, name="inverse")
        alpha_rows = held.tile([P, groups, DEG], F32, name="alpha_rows")
        pe_groups = pe_rows[:].rearrange("p (g d) -> p g d", d=DEG)
        nc.vector.reduce_max(minus_top[:], pe_groups, axis=AX.X, negate=True)
        for g in range(groups):
            nc.scalar.activation(
                expd[:, g, :], pe_groups[:, g, :], ACT.Exp,
                bias=minus_top[:, g : g + 1], accum_out=total[:, g : g + 1],
            )
        nc.vector.reciprocal(inverse[:], total[:])
        nc.vector.tensor_tensor(
            alpha_rows[:], expd[:], inverse[:].unsqueeze(2).to_broadcast([P, groups, DEG]), ALU.mult
        )

        rows_per_piece = PIECE // ROW
        alpha_pieces = []
        for r in range(PIECES):
            diagonal = spread.tile([P, rows_per_piece, ROW], F32, name="diagonal")
            nc.vector.tensor_tensor(
                diagonal[:],
                identity[:, r * rows_per_piece : (r + 1) * rows_per_piece]
                .unsqueeze(2)
                .to_broadcast([P, rows_per_piece, ROW]),
                alpha_rows[:].rearrange("p g d -> p (g d)").unsqueeze(1).to_broadcast([P, rows_per_piece, ROW]),
                ALU.mult,
            )
            alpha_bank = alpha_psum.tile([P, PIECE], F32, name="alpha_bank")
            nc.tensor.matmul(
                alpha_bank[:], ones[:], diagonal[:].rearrange("p q t -> p (q t)"), start=True, stop=True
            )
            alpha_piece = held.tile([P, PIECE], F32, name=f"alpha_piece{r}")
            nc.scalar.copy(alpha_piece[:], alpha_bank[:])
            alpha_pieces.append(alpha_piece)

        out_blocks = out.rearrange("(b p) m -> p b m", p=P)
        neighs = []
        hids = []
        first_levels = []
        for s in range(CHUNKS + 2):
            if s < CHUNKS:
                neigh = work.tile([P, CB, CHUNK], BF16, name="neigh")
                neighs.append(neigh)
                for h in range(CHUNK_PIECES):
                    r = s * CHUNK_PIECES + h
                    columns = slice(h * NODES, (h + 1) * NODES)
                    product = products.tile([P, CB, PIECE], F32, name="product")
                    terms = product[:].rearrange("p b (m d) -> p b m d", d=DEG)
                    for b in range(CB):
                        nc.vector.tensor_tensor(
                            product[:, b, :],
                            x_blocks[b][:].indirect(offsets[:, r * OFFS_COLS : (r + 1) * OFFS_COLS]),
                            alpha_pieces[r][:],
                            ALU.mult,
                        )
                        if r >= PE_PIECES and b % 2 == 1:
                            with nc.allow_low_precision(reason="summed in float32, rounded once to bfloat16"):
                                nc.vector.reduce_sum(
                                    neigh[:, b - 1 : b + 1, columns], terms[:, b - 1 : b + 1, :, :], axis=AX.X
                                )
                    if r < PE_PIECES:
                        pair_bank = sum_psum.tile([P, CB, NODES, 2], F32, name="pair_bank")
                        for i in range(DEG // 2):
                            nc.tensor.matmul(
                                pair_bank[:], identity[:], terms[:, :, :, 2 * i : 2 * i + 2],
                                start=(i == 0), stop=(i == DEG // 2 - 1),
                            )
                        pair = pairs.tile([P, 2, CB, NODES], F32, name="pair")
                        nc.scalar.copy(pair[:], pair_bank[:].rearrange("p b m e -> p e b m"))
                        first_levels.append((pair, neigh, columns))
                    if 1 <= r <= PE_PIECES:
                        pair, pair_neigh, pair_columns = first_levels[r - 1]
                        sum_bank = sum_psum.tile([P, CB, NODES], F32, name="sum_bank")
                        for e in range(2):
                            nc.tensor.matmul(sum_bank[:], identity[:], pair[:, e, :, :], start=(e == 0), stop=(e == 1))
                        nc.scalar.copy(pair_neigh[:, :, pair_columns], sum_bank[:])

            if 1 <= s <= CHUNKS:
                neigh = neighs[s - 1]
                hid_banks = [hid_psum.tile([P, CHUNK], F32, name=f"hid_bank{u}") for u in range(UB)]
                for b in range(CB):
                    for u in range(UB):
                        nc.tensor.matmul(
                            hid_banks[u][:], w1_sb[:, b, u * P : (u + 1) * P], neigh[:, b, :],
                            start=(b == 0), stop=(b == CB - 1),
                        )
                hid = work.tile([P, 2, UB, CHUNK], BF16, name="hid")
                hids.append(hid)
                for u in range(UB):
                    nc.scalar.activation(hid[:, 0, u, :], hid_banks[u][:], ACT.Relu, bias=b1_sb[:, u : u + 1])
                    nc.scalar.activation(
                        hid[:, 1, u, :], hid_banks[u][:], ACT.Relu, bias=minus_b1[:, u : u + 1], scale=-SLOPE
                    )

            if s >= 2:
                c = s - 2
                hid = hids[c]
                out_bank = out_psum.tile([P, CB, CHUNK], F32, name="out_bank")
                for b in range(CB):
                    for u in range(UB):
                        nc.tensor.matmul(
                            out_bank[:, b, :], w2_sb[:, u, b * P : (b + 1) * P], hid[:, 0, u, :],
                            start=(u == 0), stop=False,
                        )
                        nc.tensor.matmul(
                            out_bank[:, b, :], minus_w2[:, u, b * P : (b + 1) * P], hid[:, 1, u, :],
                            start=False, stop=(u == UB - 1),
                        )
                result = work.tile([P, CB, CHUNK], F32, name="result")
                for b in range(CB):
                    nc.scalar.activation(result[:, b, :], out_bank[:, b, :], ACT.Relu, bias=b2_sb[:, b : b + 1])
                nc.sync.dma_start(out_blocks[:, :, c * CHUNK : (c + 1) * CHUNK], result[:])
